import numpy as np
import ml_dtypes


BF16 = ml_dtypes.bfloat16


def bf(x):
    return np.asarray(x, np.float32).astype(BF16)


def f64(x):
    return np.asarray(x).astype(np.float64)


E2M1 = np.array([0.0, 0.5, 1.0, 1.5, 2.0, 3.0, 4.0, 6.0, -0.0, -0.5, -1.0, -1.5, -2.0, -3.0, -4.0, -6.0])


def pack_weight(w, fmt):
    k, n = w.shape
    w = f64(bf(w)).reshape(k // 32, 32, n)
    amax = np.abs(w).max(1)
    if fmt == "e4m3":
        byte = np.frexp(amax)[1] - 1 + 127 - 7
    else:
        mant, ex = np.frexp(amax / 6.0)
        byte = np.where(mant > 0.5, ex, ex - 1) + 127
    byte = np.clip(np.where(amax > 0, byte, 1), 1, 254)
    scaled = (w * np.exp2(127.0 - byte)[:, None, :]).reshape(k, n).astype(np.float32)
    by_word = np.ascontiguousarray(scaled.reshape(k // 512, 128, 4, n).transpose(0, 1, 3, 2))
    if fmt == "e4m3":
        words = by_word.astype(ml_dtypes.float8_e4m3fn).view(np.uint8)
    else:
        c = by_word.astype(ml_dtypes.float4_e2m1fn).view(np.uint8) & 0xF
        words = c[..., 0::2] | (c[..., 1::2] << 4)
    return np.ascontiguousarray(words), np.ascontiguousarray(byte.astype(np.uint8).reshape(k // 512, 16, n))


def unpack_weight(words, scales, fmt):
    g, p, n, _ = words.shape
    if fmt == "e4m3":
        vals = np.ascontiguousarray(words).view(ml_dtypes.float8_e4m3fn).astype(np.float64)
    else:
        nib = np.empty((g, p, n, 4), np.uint8)
        nib[..., 0::2] = words & 0xF
        nib[..., 1::2] = words >> 4
        vals = E2M1[nib]
    vals = vals * np.repeat(np.exp2(scales.astype(np.float64) - 127.0), 8, axis=1)[..., None]
    return vals.transpose(0, 1, 3, 2).reshape(g * 512, n)

def pack4(w):
    words, scales = pack_weight(w, "e2m1")
    return words.reshape(words.shape[0], 128, -1), scales


def unpack4(words, scales):
    return unpack_weight(words.reshape(words.shape[0], 128, -1, 2), scales, "e2m1")


def kspread(k):
    return np.exp2(np.repeat(np.random.randint(-6, 7, k // 32), 32).astype(np.float64))


B, P, D, N = 4096, 1024, 1024, 1024
MINI, MAXI, EXPONENT = 0.001, 1.0, 4


def linear_normalization(maxi, mini, target_max, target_min):
    alpha = (target_max - target_min) / (maxi - mini)
    beta = target_min - alpha * mini
    return alpha, beta


def setup_inputs():
    s = kspread(D)
    x = np.random.standard_normal((B, D)) * s
    x_dot = bf(np.random.standard_normal((B, D)) * 2.0 / np.sqrt(D))
    pos_sample = np.random.standard_normal((P, D)) * s
    words, scales = pack4(np.random.standard_normal((D, N)) * 1.5 / np.sqrt(D * N) / s[:, None])
    xt = np.ascontiguousarray(x.reshape(B, D).T)
    x_words, x_scales = pack4(xt)
    pt = np.ascontiguousarray(pos_sample.reshape(P, D).T)
    pos_sample_words, pos_sample_scales = pack4(pt)
    return {"x_words": x_words,
            "x_scales": x_scales,
            "x_dot": x_dot,
            "pos_sample_words": pos_sample_words,
            "pos_sample_scales": pos_sample_scales,
            "W_words": words,
            "W_scales": scales}


def reference(x_words, x_scales, x_dot, pos_sample_words, pos_sample_scales, W_words, W_scales):
    Wq = unpack4(W_words, W_scales)
    s_pos = unpack4(pos_sample_words, pos_sample_scales).T @ Wq
    norm_pos = np.linalg.norm(s_pos, axis=1) ** EXPONENT
    alpha, beta = linear_normalization(norm_pos.max(), norm_pos.min(), MAXI, MINI)
    scores = unpack4(x_words, x_scales).T @ Wq
    norm_power = np.linalg.norm(scores, axis=1) ** EXPONENT
    scale = alpha * norm_power + beta
    xd = f64(x_dot)
    return scale * np.sum(xd * xd, axis=1)

@@ -1,0 +1,236 @@
+from contextlib import ExitStack
+
+import concourse.mybir as mybir
+from concourse.masks import make_identity
+
+F32 = mybir.dt.float32
+BF16 = mybir.dt.bfloat16
+I32 = mybir.dt.int32
+U8 = mybir.dt.uint8
+FP4X4 = mybir.dt.float4_e2m1fn_x4
+ALU = mybir.AluOpType
+ACT = mybir.ActivationFunctionType
+AX = mybir.AxisListType
+
+P = 128
+D = 1024
+N = 1024
+B = 4096
+POS = 1024
+PASSES = 2
+HALF = 512
+MINI, MAXI = 0.001, 1.0
+FLOPS = 2 * (B + POS) * D * N + 2 * (B + POS) * N + 2 * B * D
+
+POS_TILES = POS // P
+X_TILES = B // P
+STEPS = POS_TILES + X_TILES
+X_CHUNK = 2048
+XDOT_CHUNKS = [2, 2, 4, 4, 4, 4, 4, 4, 4]
+HEAD_XDOT = 3
+CALIB_STEP = 18
+
+
+def load_scales(nc, plane, scales):
+    for q in range(4):
+        nc.sync.dma_start(
+            out=plane[32 * q : 32 * q + 4, :, :].bitcast(I32),
+            in_=scales[:, 4 * q : 4 * q + 4, :].rearrange("g r n -> r g n").bitcast(I32),
+        )
+
+
+def load_codes(nc, codes, words):
+    nc.sync.dma_start(out=codes[:].bitcast(I32), in_=words.rearrange("g p n -> p g n").bitcast(I32))
+
+
+def tile_scoremagnitudemetric_kernel(
+    tc, x_words, x_scales, x_dot, pos_words, pos_scales, w_words, w_scales, out
+):
+    nc = tc.nc
+    with ExitStack() as ctx:
+        keep = ctx.enter_context(tc.tile_pool(name="keep", bufs=1))
+        scrap = ctx.enter_context(tc.tile_pool(name="scrap", bufs=3))
+        small = ctx.enter_context(tc.tile_pool(name="small", bufs=1))
+        psum = ctx.enter_context(tc.psum_pool(name="psum", bufs=4))
+        ctx.enter_context(tc.manual_schedule())
+
+        w_codes = [keep.tile([P, PASSES, 2 * HALF], U8, name="w_codes%d" % h, align_bytes=64) for h in range(2)]
+        w_plane = keep.tile([P, PASSES, N], U8, name="w_plane", align_bytes=64)
+        pos_codes = [keep.tile([P, PASSES, POS], U8, name="pos_codes%d" % h, align_bytes=64) for h in range(2)]
+        pos_plane = keep.tile([P, PASSES, POS], U8, name="pos_plane", align_bytes=64)
+        x_codes = [keep.tile([P, PASSES, 2 * X_CHUNK], U8, name="x_codes%d" % c, align_bytes=64) for c in range(2)]
+        x_plane = [keep.tile([P, PASSES, X_CHUNK], U8, name="x_plane%d" % c, align_bytes=64) for c in range(2)]
+        xdot_sb = [keep.tile([P, n, D], BF16, name="xdot%d" % c, align_bytes=64) for c, n in enumerate(XDOT_CHUNKS)]
+        xdot_tile = [sb[:, j, :] for sb, n in zip(xdot_sb, XDOT_CHUNKS) for j in range(n)]
+
+        ident = keep.tile([P, P], F32, name="ident", align_bytes=64)
+        warm = small.tile([P, 1], F32, name="warm")
+        pos_a = small.tile([P, POS_TILES], F32, name="pos_a")
+        pos_st = small.tile([P, POS_TILES, 6], F32, name="pos_st")
+        x_a = small.tile([P, X_TILES + 1], F32, name="x_a")
+        x_st = small.tile([P, X_TILES, 6], F32, name="x_st")
+        xd = small.tile([P, X_TILES], F32, name="xd")
+        xd_st = small.tile([P, X_TILES, 6], F32, name="xd_st")
+        pw = small.tile([P, X_TILES], F32, name="pw")
+        result = keep.tile([P, P], F32, name="result", align_bytes=64)
+        ab = small.tile([P, 2], F32, name="ab")
+        alpha, beta = ab[:, 0:1], ab[:, 1:2]
+
+        nc.vector.memset(warm[:], 1.0)
+        for plane in [w_plane, pos_plane] + x_plane:
+            nc.vector.memset(plane[:].rearrange("p g n -> p (g n)").bitcast(I32), 0)
+        nc.vector.memset(result[:], 0.0)
+        nc.scalar.activation(out=warm[:], in_=warm[:], func=ACT.Square)
+
+        load_codes(nc, w_codes[0], w_words[:, :, 0 : 2 * HALF])
+        load_codes(nc, pos_codes[0], pos_words[:, :, 0:POS])
+        load_scales(nc, w_plane, w_scales)
+        load_scales(nc, pos_plane, pos_scales)
+        load_codes(nc, w_codes[1], w_words[:, :, 2 * HALF :])
+        load_codes(nc, pos_codes[1], pos_words[:, :, POS:])
+        for c in range(2):
+            load_scales(nc, x_plane[c], x_scales[:, :, X_CHUNK * c : X_CHUNK * (c + 1)])
+            load_codes(nc, x_codes[c], x_words[:, :, 2 * X_CHUNK * c : 2 * X_CHUNK * (c + 1)])
+        t0 = 0
+        xdot_rows = x_dot.rearrange("(i p) d -> p i d", p=P)
+        for sb, n in zip(xdot_sb, XDOT_CHUNKS):
+            nc.gpsimd.dma_start(out=sb[:], in_=xdot_rows[:, t0 : t0 + n, :])
+            t0 += n
+        make_identity(nc, ident[:])
+
+        def matmuls(step, h, acc):
+            if step < POS_TILES:
+                codes, plane, col, pcol = pos_codes[step // 4], pos_plane, step % 4, step
+            else:
+                t = step - POS_TILES
+                codes, plane, col, pcol = x_codes[t // 16], x_plane[t // 16], t % 16, t % 16
+            for g in range(PASSES):
+                nc.tensor.matmul_mx(
+                    out=acc[:],
+                    lhsT=codes[:, g, 2 * P * col : 2 * P * (col + 1)].bitcast(FP4X4),
+                    lhsT_scale=plane[:, g, P * pcol : P * (pcol + 1)],
+                    rhs=w_codes[h][:, g, :].bitcast(FP4X4),
+                    rhs_scale=w_plane[:, g, HALF * h : HALF * (h + 1)],
+                    start=(g == 0),
+                    stop=(g == PASSES - 1),
+                )
+
+        def scalar_sumsq(src, dst):
+            junk = scrap.tile([P, D], BF16, name="junk")
+            nc.scalar.activation(out=junk[:, 0 : src.shape[1]], in_=src, func=ACT.Square, accum_out=dst)
+
+        def vector_xdot(j):
+            for h in range(2):
+                nc.vector.bn_stats(out=xd_st[:, 2 * (j // 2) + h, :], in_=xdot_tile[j][:, HALF * h : HALF * (h + 1)])
+
+        def sums_of_stats(name, stats):
+            k = stats.shape[1]
+            q = small.tile([P, k, 2], F32, name=name)
+            chores = [
+                lambda: nc.vector.tensor_tensor(out=q[:], in0=stats[:, :, 1::3], in1=stats[:, :, 1::3], op=ALU.mult),
+                lambda: nc.vector.scalar_tensor_tensor(
+                    out=q[:], in0=q[:], scalar=float(HALF // 2), in1=stats[:, :, 2::3], op0=ALU.mult, op1=ALU.add
+                ),
+            ]
+            return q, chores
+
+        def powers(name, stats, scalar_sums, dst):
+            q, chores = sums_of_stats(name, stats)
+            return chores + [
+                lambda: nc.vector.tensor_tensor(out=q[:, :, 0], in0=q[:, :, 0], in1=q[:, :, 1], op=ALU.add),
+                lambda: nc.vector.tensor_tensor(out=q[:, :, 0], in0=q[:, :, 0], in1=scalar_sums, op=ALU.add),
+                lambda: nc.vector.tensor_tensor(out=dst, in0=q[:, :, 0], in1=q[:, :, 0], op=ALU.mult),
+            ]
+
+        chores = {}
+
+        def at(step, per_step, todo):
+            for k, chore in enumerate(todo):
+                chores.setdefault(step + k // per_step, []).append(chore)
+
+        pos_pw = small.tile([P, POS_TILES], F32, name="pos_pw")
+        ends = small.tile([P, 2], F32, name="ends")
+        span = small.tile([P, 4], F32, name="span")
+        at(8, 2, powers("pos_q", pos_st[:], pos_a[:], pos_pw[:]) + [
+            lambda: nc.vector.tensor_reduce(out=ends[:, 0:1], in_=pos_pw[:], axis=AX.X, op=ALU.max),
+            lambda: nc.vector.tensor_reduce(out=ends[:, 1:2], in_=pos_pw[:], axis=AX.X, op=ALU.min),
+        ])
+        spread = {}
+
+        def spread_ends():
+            spread[0] = psum.tile([P, 2, P], F32, name="acc_v")
+            for k in range(2):
+                nc.tensor.transpose(spread[0][:, k, :], ends[:, k : k + 1].to_broadcast([P, P]), ident[:])
+
+        at(CALIB_STEP, 2, [
+            lambda: nc.vector.tensor_reduce(out=span[:, 0:1], in_=spread[0][:, 0, :], axis=AX.X, op=ALU.max),
+            lambda: nc.vector.tensor_reduce(out=span[:, 1:2], in_=spread[0][:, 1, :], axis=AX.X, op=ALU.min),
+            lambda: nc.vector.tensor_tensor(out=span[:, 2:3], in0=span[:, 0:1], in1=span[:, 1:2], op=ALU.subtract),
+            lambda: nc.vector.reciprocal(out=span[:, 3:4], in_=span[:, 2:3]),
+            lambda: nc.vector.tensor_scalar(out=alpha, in0=span[:, 3:4], scalar1=MAXI - MINI, scalar2=None, op0=ALU.mult),
+            lambda: nc.vector.tensor_tensor(out=span[:, 2:3], in0=alpha, in1=span[:, 1:2], op=ALU.mult),
+            lambda: nc.vector.tensor_scalar(out=beta, in0=span[:, 2:3], scalar1=-1.0, scalar2=MINI, op0=ALU.mult, op1=ALU.add),
+        ])
+
+        def finish(lo, hi):
+            return [
+                lambda: nc.vector.tensor_scalar(
+                    out=pw[:, lo:hi], in0=pw[:, lo:hi], scalar1=alpha, scalar2=beta, op0=ALU.mult, op1=ALU.add
+                ),
+                lambda: nc.vector.tensor_tensor(out=result[:, lo:hi], in0=pw[:, lo:hi], in1=xd[:, lo:hi], op=ALU.mult),
+            ]
+
+        at(25, 1, powers("q1", x_st[:, 0:16, :], x_a[:, 0:16], pw[:, 0:16]))
+        last = X_TILES - 1
+        xd_q, xd_chores = sums_of_stats("xd_q", xd_st[:])
+        last_scale = small.tile([P, 2], F32, name="last_scale")
+        at(36, 4, xd_chores + [
+            lambda: nc.vector.tensor_reduce(
+                out=xd[:, 1::2], in_=xd_q[:].rearrange("p (k h) e -> p k (h e)", h=2), axis=AX.X, op=ALU.add
+            )
+        ] + powers("q2", x_st[:, 16:28, :], x_a[:, 16:28], pw[:, 16:28]) + [
+            lambda: nc.vector.tensor_tensor(out=last_scale[:, 0:1], in0=alpha, in1=xd[:, last : last + 1], op=ALU.mult),
+            lambda: nc.vector.tensor_tensor(out=last_scale[:, 1:2], in0=beta, in1=xd[:, last : last + 1], op=ALU.mult),
+        ] + finish(0, 28))
+        tail = powers("q3", x_st[:, 28:31, :], x_a[:, 28:31], pw[:, 28:31]) + finish(28, 31)
+
+        for k in range(HEAD_XDOT):
+            scalar_sumsq(xdot_tile[2 * k], xd[:, 2 * k : 2 * k + 1])
+            vector_xdot(2 * k + 1)
+        rest = X_TILES // 2 - HEAD_XDOT
+        span_steps = 35
+        for step in range(STEPS):
+            t = step - POS_TILES
+            if step == CALIB_STEP:
+                spread_ends()
+            acc_s = psum.tile([P, HALF], F32, name="acc_s")
+            matmuls(step, 0, acc_s)
+            scalar_sumsq(acc_s[:], pos_a[:, step : step + 1] if t < 0 else x_a[:, t : t + 1])
+            if t < last:
+                acc_v = psum.tile([P, HALF], F32, name="acc_v")
+                matmuls(step, 1, acc_v)
+                nc.vector.bn_stats(out=pos_st[:, step, :] if t < 0 else x_st[:, t, :], in_=acc_v[:])
+            else:
+                acc_s = psum.tile([P, HALF], F32, name="acc_s")
+                matmuls(step, 1, acc_s)
+                scalar_sumsq(acc_s[:], x_a[:, t + 1 : t + 2])
+            if step < span_steps and (step + 1) * rest // span_steps > step * rest // span_steps:
+                k = HEAD_XDOT + step * rest // span_steps
+                scalar_sumsq(xdot_tile[2 * k], xd[:, 2 * k : 2 * k + 1])
+                vector_xdot(2 * k + 1)
+            for chore in chores.get(step, []):
+                chore()
+        for chore in tail:
+            chore()
+        nc.scalar.activation(
+            out=pw[:, last : last + 1], in_=x_a[:, last : last + 1], func=ACT.Square, bias=x_a[:, last + 1 : last + 2]
+        )
+        nc.scalar.activation(
+            out=result[:, last : last + 1], in_=pw[:, last : last + 1], func=ACT.Identity,
+            scale=last_scale[:, 0:1], bias=last_scale[:, 1:2],
+        )
+        turned = psum.tile([P, P], F32, name="acc_v")
+        nc.tensor.transpose(turned[:], result[:], ident[:])
+        rows = small.tile([X_TILES, P], F32, name="rows")
+        nc.scalar.copy(out=rows[:], in_=turned[0:X_TILES, :])
+        nc.sync.dma_start(out=out.rearrange("(i p) -> i p", p=P), in_=rows[:])

@@ -25,10 +25,17 @@ FLOPS = 2 * (B + POS) * D * N + 2 * (B + POS) * N + 2 * B * D
 POS_TILES = POS // P
 X_TILES = B // P
 STEPS = POS_TILES + X_TILES
+LAST = X_TILES - 1
+LATE = 29
+N_LATE = X_TILES - LATE
 X_CHUNK = 2048
 XDOT_CHUNKS = [2, 2, 4, 4, 4, 4, 4, 4, 4]
-HEAD_XDOT = 3
-CALIB_STEP = 18
+GPSIMD_CHUNKS = 3
+CALIB_STEP = 20
+WARM = 9
+S_XDOT = [0, 2, 4]
+V_XDOT = [j for j in range(X_TILES) if j not in S_XDOT]
+V_TILES = list(range(2, 28, 4))
 
 
 def load_scales(nc, plane, scales):
@@ -50,8 +57,7 @@ def tile_scoremagnitudemetric_kernel(
     with ExitStack() as ctx:
         keep = ctx.enter_context(tc.tile_pool(name="keep", bufs=1))
         scrap = ctx.enter_context(tc.tile_pool(name="scrap", bufs=3))
-        small = ctx.enter_context(tc.tile_pool(name="small", bufs=1))
-        psum = ctx.enter_context(tc.psum_pool(name="psum", bufs=4))
+        psum = ctx.enter_context(tc.psum_pool(name="psum", bufs=1))
         ctx.enter_context(tc.manual_schedule())
 
         w_codes = [keep.tile([P, PASSES, 2 * HALF], U8, name="w_codes%d" % h, align_bytes=64) for h in range(2)]
@@ -59,28 +65,47 @@ def tile_scoremagnitudemetric_kernel(
         pos_codes = [keep.tile([P, PASSES, POS], U8, name="pos_codes%d" % h, align_bytes=64) for h in range(2)]
         pos_plane = keep.tile([P, PASSES, POS], U8, name="pos_plane", align_bytes=64)
         x_codes = [keep.tile([P, PASSES, 2 * X_CHUNK], U8, name="x_codes%d" % c, align_bytes=64) for c in range(2)]
-        x_plane = [keep.tile([P, PASSES, X_CHUNK], U8, name="x_plane%d" % c, align_bytes=64) for c in range(2)]
+        x_plane = keep.tile([P, PASSES, B], U8, name="x_plane", align_bytes=64)
         xdot_sb = [keep.tile([P, n, D], BF16, name="xdot%d" % c, align_bytes=64) for c, n in enumerate(XDOT_CHUNKS)]
         xdot_tile = [sb[:, j, :] for sb, n in zip(xdot_sb, XDOT_CHUNKS) for j in range(n)]
 
         ident = keep.tile([P, P], F32, name="ident", align_bytes=64)
-        warm = small.tile([P, 1], F32, name="warm")
-        pos_a = small.tile([P, POS_TILES], F32, name="pos_a")
-        pos_st = small.tile([P, POS_TILES, 6], F32, name="pos_st")
-        x_a = small.tile([P, X_TILES + 1], F32, name="x_a")
-        x_st = small.tile([P, X_TILES, 6], F32, name="x_st")
-        xd = small.tile([P, X_TILES], F32, name="xd")
-        xd_st = small.tile([P, X_TILES, 6], F32, name="xd_st")
-        pw = small.tile([P, X_TILES], F32, name="pw")
+        zeros = keep.tile([P, HALF // 2], F32, name="zeros", align_bytes=64)
         result = keep.tile([P, P], F32, name="result", align_bytes=64)
-        ab = small.tile([P, 2], F32, name="ab")
+        warm = keep.tile([P, 1], F32, name="warm")
+        pos_ab = keep.tile([P, POS_TILES, 2], F32, name="pos_ab")
+        pos_st = keep.tile([P, POS_TILES, 6], F32, name="pos_st")
+        pos_q = keep.tile([P, POS_TILES, 2], F32, name="pos_q")
+        pos_pw = keep.tile([P, POS_TILES], F32, name="pos_pw")
+        ends = keep.tile([P, 2], F32, name="ends")
+        span = keep.tile([P, 4], F32, name="span")
+        ab = keep.tile([P, 2], F32, name="ab")
+        x_ab = keep.tile([P, X_TILES, 2], F32, name="x_ab")
+        x_st = keep.tile([P, len(V_TILES), 6], F32, name="x_st")
+        x_q = keep.tile([P, len(V_TILES), 2], F32, name="x_q")
+        x_end = keep.tile([P, 1], F32, name="x_end")
+        xd = keep.tile([P, X_TILES], F32, name="xd")
+        pw = keep.tile([P, X_TILES], F32, name="pw")
+        late_ax = keep.tile([P, N_LATE], F32, name="late_ax")
+        late_bx = keep.tile([P, N_LATE], F32, name="late_bx")
+        late_ss = keep.tile([P, N_LATE], F32, name="late_ss")
+        pw_last = keep.tile([P, 1], F32, name="pw_last")
+        rows = keep.tile([X_TILES, P], F32, name="rows")
         alpha, beta = ab[:, 0:1], ab[:, 1:2]
 
+        nc.gpsimd.memset(zeros[:], 0.0)
+        nc.vector.memset(w_plane[:].rearrange("p g n -> p (g n)").bitcast(I32), 0)
+        nc.vector.memset(pos_plane[:].rearrange("p g n -> p (g n)").bitcast(I32), 0)
         nc.vector.memset(warm[:], 1.0)
-        for plane in [w_plane, pos_plane] + x_plane:
-            nc.vector.memset(plane[:].rearrange("p g n -> p (g n)").bitcast(I32), 0)
+        nc.vector.memset(x_plane[:].rearrange("p g n -> p (g n)").bitcast(I32), 0)
         nc.vector.memset(result[:], 0.0)
         nc.scalar.activation(out=warm[:], in_=warm[:], func=ACT.Square)
+
+        xdot_rows = x_dot.rearrange("(i p) d -> p i d", p=P)
+        first = [sum(XDOT_CHUNKS[:c]) for c in range(len(XDOT_CHUNKS))]
+
+        def load_xdot(eng, c):
+            eng.dma_start(out=xdot_sb[c][:], in_=xdot_rows[:, first[c] : first[c] + XDOT_CHUNKS[c], :])
 
         load_codes(nc, w_codes[0], w_words[:, :, 0 : 2 * HALF])
         load_codes(nc, pos_codes[0], pos_words[:, :, 0:POS])
@@ -88,58 +113,79 @@ def tile_scoremagnitudemetric_kernel(
         load_scales(nc, pos_plane, pos_scales)
         load_codes(nc, w_codes[1], w_words[:, :, 2 * HALF :])
         load_codes(nc, pos_codes[1], pos_words[:, :, POS:])
-        for c in range(2):
-            load_scales(nc, x_plane[c], x_scales[:, :, X_CHUNK * c : X_CHUNK * (c + 1)])
-            load_codes(nc, x_codes[c], x_words[:, :, 2 * X_CHUNK * c : 2 * X_CHUNK * (c + 1)])
-        t0 = 0
-        xdot_rows = x_dot.rearrange("(i p) d -> p i d", p=P)
-        for sb, n in zip(xdot_sb, XDOT_CHUNKS):
-            nc.gpsimd.dma_start(out=sb[:], in_=xdot_rows[:, t0 : t0 + n, :])
-            t0 += n
+        load_scales(nc, x_plane, x_scales)
+        load_codes(nc, x_codes[0], x_words[:, :, 0 : 2 * X_CHUNK])
+        load_xdot(nc.sync, GPSIMD_CHUNKS)
+        load_codes(nc, x_codes[1], x_words[:, :, 2 * X_CHUNK :])
+        for c in range(GPSIMD_CHUNKS + 1, len(XDOT_CHUNKS)):
+            load_xdot(nc.sync, c)
+        for c in range(GPSIMD_CHUNKS):
+            load_xdot(nc.gpsimd, c)
         make_identity(nc, ident[:])
 
-        def matmuls(step, h, acc):
+        def psum_s(n=HALF):
+            return psum.tile([P, n], F32, name="acc_s", bufs=5)
+
+        def psum_v(shape):
+            return psum.tile(shape, F32, name="acc_v", bufs=3)
+
+        idle = psum_v([P, HALF])
+        for k in range(WARM):
+            nc.tensor.matmul(idle[:], zeros[:].bitcast(BF16)[:, 0:P], zeros[:].bitcast(BF16), start=True, stop=True)
+
+        def matmuls(step, h, acc, lo=0, n=HALF):
             if step < POS_TILES:
                 codes, plane, col, pcol = pos_codes[step // 4], pos_plane, step % 4, step
             else:
                 t = step - POS_TILES
-                codes, plane, col, pcol = x_codes[t // 16], x_plane[t // 16], t % 16, t % 16
+                codes, plane, col, pcol = x_codes[t // 16], x_plane, t % 16, t
             for g in range(PASSES):
                 nc.tensor.matmul_mx(
                     out=acc[:],
                     lhsT=codes[:, g, 2 * P * col : 2 * P * (col + 1)].bitcast(FP4X4),
                     lhsT_scale=plane[:, g, P * pcol : P * (pcol + 1)],
-                    rhs=w_codes[h][:, g, :].bitcast(FP4X4),
-                    rhs_scale=w_plane[:, g, HALF * h : HALF * (h + 1)],
+                    rhs=w_codes[h][:, g, 2 * lo : 2 * (lo + n)].bitcast(FP4X4),
+                    rhs_scale=w_plane[:, g, HALF * h + lo : HALF * h + lo + n],
                     start=(g == 0),
                     stop=(g == PASSES - 1),
                 )
 
         def scalar_sumsq(src, dst):
-            junk = scrap.tile([P, D], BF16, name="junk")
+            junk = scrap.tile([P, D], BF16, name="junk_s")
             nc.scalar.activation(out=junk[:, 0 : src.shape[1]], in_=src, func=ACT.Square, accum_out=dst)
 
         def vector_xdot(j):
-            for h in range(2):
-                nc.vector.bn_stats(out=xd_st[:, 2 * (j // 2) + h, :], in_=xdot_tile[j][:, HALF * h : HALF * (h + 1)])
+            junk = scrap.tile([P, D], F32, name="junk_v")
+            nc.vector.scalar_tensor_tensor(
+                out=junk[:], in0=xdot_tile[j], scalar=1.0, in1=xdot_tile[j], op0=ALU.mult, op1=ALU.mult,
+                accum_out=xd[:, j : j + 1],
+            )
 
-        def sums_of_stats(name, stats):
-            k = stats.shape[1]
-            q = small.tile([P, k, 2], F32, name=name)
-            chores = [
-                lambda: nc.vector.tensor_tensor(out=q[:], in0=stats[:, :, 1::3], in1=stats[:, :, 1::3], op=ALU.mult),
+        def scalar_half(step, h, dst, lo=0, n=HALF):
+            acc_s = psum_s(n)
+            matmuls(step, h, acc_s, lo, n)
+            scalar_sumsq(acc_s[:], dst)
+
+        def vector_half(step, h, dst):
+            acc_v = psum_v([P, HALF])
+            matmuls(step, h, acc_v)
+            nc.vector.bn_stats(out=dst, in_=acc_v[:])
+
+        tt = nc.vector.tensor_tensor
+
+        def sums_of_stats(stats, q, dst):
+            return [
+                lambda: tt(out=q, in0=stats[:, :, 1::3], in1=stats[:, :, 1::3], op=ALU.mult),
                 lambda: nc.vector.scalar_tensor_tensor(
-                    out=q[:], in0=q[:], scalar=float(HALF // 2), in1=stats[:, :, 2::3], op0=ALU.mult, op1=ALU.add
+                    out=q, in0=q, scalar=float(HALF // 2), in1=stats[:, :, 2::3], op0=ALU.mult, op1=ALU.add
                 ),
+                lambda: tt(out=dst, in0=q[:, :, 0], in1=q[:, :, 1], op=ALU.add),
             ]
-            return q, chores
 
-        def powers(name, stats, scalar_sums, dst):
-            q, chores = sums_of_stats(name, stats)
-            return chores + [
-                lambda: nc.vector.tensor_tensor(out=q[:, :, 0], in0=q[:, :, 0], in1=q[:, :, 1], op=ALU.add),
-                lambda: nc.vector.tensor_tensor(out=q[:, :, 0], in0=q[:, :, 0], in1=scalar_sums, op=ALU.add),
-                lambda: nc.vector.tensor_tensor(out=dst, in0=q[:, :, 0], in1=q[:, :, 0], op=ALU.mult),
+        def powers(sums, dst):
+            return [
+                lambda: tt(out=dst, in0=sums[:, :, 0], in1=sums[:, :, 1], op=ALU.add),
+                lambda: tt(out=dst, in0=dst, in1=dst, op=ALU.mult),
             ]
 
         chores = {}
@@ -148,89 +194,87 @@ def tile_scoremagnitudemetric_kernel(
             for k, chore in enumerate(todo):
                 chores.setdefault(step + k // per_step, []).append(chore)
 
-        pos_pw = small.tile([P, POS_TILES], F32, name="pos_pw")
-        ends = small.tile([P, 2], F32, name="ends")
-        span = small.tile([P, 4], F32, name="span")
-        at(8, 2, powers("pos_q", pos_st[:], pos_a[:], pos_pw[:]) + [
-            lambda: nc.vector.tensor_reduce(out=ends[:, 0:1], in_=pos_pw[:], axis=AX.X, op=ALU.max),
-            lambda: nc.vector.tensor_reduce(out=ends[:, 1:2], in_=pos_pw[:], axis=AX.X, op=ALU.min),
-        ])
         spread = {}
 
         def spread_ends():
-            spread[0] = psum.tile([P, 2, P], F32, name="acc_v")
+            spread[0] = psum_v([P, 2, P])
             for k in range(2):
                 nc.tensor.transpose(spread[0][:, k, :], ends[:, k : k + 1].to_broadcast([P, P]), ident[:])
 
-        at(CALIB_STEP, 2, [
+        at(8, 1, sums_of_stats(pos_st[:], pos_q[:], pos_ab[:, :, 1]) + powers(pos_ab[:], pos_pw[:]) + [
+            lambda: nc.vector.tensor_reduce(out=ends[:, 0:1], in_=pos_pw[:], axis=AX.X, op=ALU.max),
+            lambda: nc.vector.tensor_reduce(out=ends[:, 1:2], in_=pos_pw[:], axis=AX.X, op=ALU.min),
+        ])
+        at(CALIB_STEP, 1, [
             lambda: nc.vector.tensor_reduce(out=span[:, 0:1], in_=spread[0][:, 0, :], axis=AX.X, op=ALU.max),
             lambda: nc.vector.tensor_reduce(out=span[:, 1:2], in_=spread[0][:, 1, :], axis=AX.X, op=ALU.min),
-            lambda: nc.vector.tensor_tensor(out=span[:, 2:3], in0=span[:, 0:1], in1=span[:, 1:2], op=ALU.subtract),
+            lambda: tt(out=span[:, 2:3], in0=span[:, 0:1], in1=span[:, 1:2], op=ALU.subtract),
             lambda: nc.vector.reciprocal(out=span[:, 3:4], in_=span[:, 2:3]),
             lambda: nc.vector.tensor_scalar(out=alpha, in0=span[:, 3:4], scalar1=MAXI - MINI, scalar2=None, op0=ALU.mult),
-            lambda: nc.vector.tensor_tensor(out=span[:, 2:3], in0=alpha, in1=span[:, 1:2], op=ALU.mult),
+            lambda: tt(out=span[:, 2:3], in0=alpha, in1=span[:, 1:2], op=ALU.mult),
             lambda: nc.vector.tensor_scalar(out=beta, in0=span[:, 2:3], scalar1=-1.0, scalar2=MINI, op0=ALU.mult, op1=ALU.add),
         ])
+        at(35, 2, sums_of_stats(x_st[:], x_q[:], x_ab[:, 2:28:4, 1]) + [
+            lambda: nc.vector.tensor_scalar(out=late_ax[:], in0=xd[:, LATE:], scalar1=alpha, scalar2=None, op0=ALU.mult),
+            lambda: nc.vector.tensor_scalar(out=late_bx[:], in0=xd[:, LATE:], scalar1=beta, scalar2=None, op0=ALU.mult),
+        ])
+        at(37, 4, powers(x_ab[:, 0:LATE, :], pw[:, 0:LATE]) + [
+            lambda: nc.vector.tensor_scalar(
+                out=pw[:, 0:LATE], in0=pw[:, 0:LATE], scalar1=alpha, scalar2=beta, op0=ALU.mult, op1=ALU.add
+            ),
+            lambda: tt(out=result[:, 0:LATE], in0=pw[:, 0:LATE], in1=xd[:, 0:LATE], op=ALU.mult),
+        ])
 
-        def finish(lo, hi):
-            return [
-                lambda: nc.vector.tensor_scalar(
-                    out=pw[:, lo:hi], in0=pw[:, lo:hi], scalar1=alpha, scalar2=beta, op0=ALU.mult, op1=ALU.add
-                ),
-                lambda: nc.vector.tensor_tensor(out=result[:, lo:hi], in0=pw[:, lo:hi], in1=xd[:, lo:hi], op=ALU.mult),
-            ]
+        def late_tile(t):
+            k = t - LATE
+            ss = late_ss[:, k : k + 1]
+            tt(out=ss, in0=x_ab[:, t, 0:1], in1=x_ab[:, t, 1:2], op=ALU.add)
+            if t < LAST:
+                nc.vector.scalar_tensor_tensor(out=ss, in0=ss, scalar=ss, in1=late_ax[:, k : k + 1], op0=ALU.mult, op1=ALU.mult)
+                tt(out=result[:, t : t + 1], in0=ss, in1=late_bx[:, k : k + 1], op=ALU.add)
 
-        at(25, 1, powers("q1", x_st[:, 0:16, :], x_a[:, 0:16], pw[:, 0:16]))
-        last = X_TILES - 1
-        xd_q, xd_chores = sums_of_stats("xd_q", xd_st[:])
-        last_scale = small.tile([P, 2], F32, name="last_scale")
-        at(36, 4, xd_chores + [
-            lambda: nc.vector.tensor_reduce(
-                out=xd[:, 1::2], in_=xd_q[:].rearrange("p (k h) e -> p k (h e)", h=2), axis=AX.X, op=ALU.add
-            )
-        ] + powers("q2", x_st[:, 16:28, :], x_a[:, 16:28], pw[:, 16:28]) + [
-            lambda: nc.vector.tensor_tensor(out=last_scale[:, 0:1], in0=alpha, in1=xd[:, last : last + 1], op=ALU.mult),
-            lambda: nc.vector.tensor_tensor(out=last_scale[:, 1:2], in0=beta, in1=xd[:, last : last + 1], op=ALU.mult),
-        ] + finish(0, 28))
-        tail = powers("q3", x_st[:, 28:31, :], x_a[:, 28:31], pw[:, 28:31]) + finish(28, 31)
+        for j in S_XDOT:
+            scalar_sumsq(xdot_tile[j], xd[:, j : j + 1])
+        for j in V_XDOT[:2]:
+            vector_xdot(j)
+        slots = {}
+        for k, j in enumerate(V_XDOT[2:6]):
+            slots.setdefault(1 + 2 * k, []).append(j)
+        for k, j in enumerate(V_XDOT[6:]):
+            slots.setdefault(8 + k * 27 // len(V_XDOT[6:]), []).append(j)
 
-        for k in range(HEAD_XDOT):
-            scalar_sumsq(xdot_tile[2 * k], xd[:, 2 * k : 2 * k + 1])
-            vector_xdot(2 * k + 1)
-        rest = X_TILES // 2 - HEAD_XDOT
-        span_steps = 35
+        for step in range(4):
+            scalar_half(step, 0, pos_ab[:, step, 0:1])
         for step in range(STEPS):
             t = step - POS_TILES
             if step == CALIB_STEP:
                 spread_ends()
-            acc_s = psum.tile([P, HALF], F32, name="acc_s")
-            matmuls(step, 0, acc_s)
-            scalar_sumsq(acc_s[:], pos_a[:, step : step + 1] if t < 0 else x_a[:, t : t + 1])
-            if t < last:
-                acc_v = psum.tile([P, HALF], F32, name="acc_v")
-                matmuls(step, 1, acc_v)
-                nc.vector.bn_stats(out=pos_st[:, step, :] if t < 0 else x_st[:, t, :], in_=acc_v[:])
+            if t < 0:
+                if step >= 4:
+                    scalar_half(step, 0, pos_ab[:, step, 0:1])
+                vector_half(step, 1, pos_st[:, step, :])
             else:
-                acc_s = psum.tile([P, HALF], F32, name="acc_s")
-                matmuls(step, 1, acc_s)
-                scalar_sumsq(acc_s[:], x_a[:, t + 1 : t + 2])
-            if step < span_steps and (step + 1) * rest // span_steps > step * rest // span_steps:
-                k = HEAD_XDOT + step * rest // span_steps
-                scalar_sumsq(xdot_tile[2 * k], xd[:, 2 * k : 2 * k + 1])
-                vector_xdot(2 * k + 1)
+                scalar_half(step, 0, x_ab[:, t, 0:1])
+                if t in V_TILES:
+                    vector_half(step, 1, x_st[:, V_TILES.index(t), :])
+                elif t < LAST:
+                    scalar_half(step, 1, x_ab[:, t, 1:2])
+                else:
+                    scalar_half(step, 1, x_ab[:, t, 1:2], 0, HALF // 2)
+                    scalar_half(step, 1, x_end[:], HALF // 2, HALF // 2)
+            for j in slots.get(step, []):
+                vector_xdot(j)
             for chore in chores.get(step, []):
                 chore()
-        for chore in tail:
-            chore()
+            if t >= LATE:
+                late_tile(t)
+        k = N_LATE - 1
+        nc.scalar.activation(out=pw_last[:], in_=x_end[:], func=ACT.Square, bias=late_ss[:, k : k + 1])
         nc.scalar.activation(
-            out=pw[:, last : last + 1], in_=x_a[:, last : last + 1], func=ACT.Square, bias=x_a[:, last + 1 : last + 2]
+            out=result[:, LAST : LAST + 1], in_=pw_last[:], func=ACT.Identity,
+            scale=late_ax[:, k : k + 1], bias=late_bx[:, k : k + 1],
         )
-        nc.scalar.activation(
-            out=result[:, last : last + 1], in_=pw[:, last : last + 1], func=ACT.Identity,
-            scale=last_scale[:, 0:1], bias=last_scale[:, 1:2],
-        )
-        turned = psum.tile([P, P], F32, name="acc_v")
+        turned = psum_v([P, P])
         nc.tensor.transpose(turned[:], result[:], ident[:])
-        rows = small.tile([X_TILES, P], F32, name="rows")
         nc.scalar.copy(out=rows[:], in_=turned[0:X_TILES, :])
-        nc.sync.dma_start(out=out.rearrange("(i p) -> i p", p=P), in_=rows[:])
+        nc.scalar.dma_start(out=out.rearrange("(i p) -> i p", p=P), in_=rows[:])

@@ -26,16 +26,17 @@ POS_TILES = POS // P
 X_TILES = B // P
 STEPS = POS_TILES + X_TILES
 LAST = X_TILES - 1
-LATE = 29
+LATE = 24
 N_LATE = X_TILES - LATE
 X_CHUNK = 2048
 XDOT_CHUNKS = [2, 2, 4, 4, 4, 4, 4, 4, 4]
 GPSIMD_CHUNKS = 3
-CALIB_STEP = 20
+CALIB_STEP = 24
 WARM = 9
-S_XDOT = [0, 2, 4]
-V_XDOT = [j for j in range(X_TILES) if j not in S_XDOT]
-V_TILES = list(range(2, 28, 4))
+FOLD = 32
+G_XDOT = [0, 4, 8, 12, 16]
+S_XDOT = [j for j in range(X_TILES) if j not in G_XDOT]
+S_HEAD = 3
 
 
 def load_scales(nc, plane, scales):
@@ -60,6 +61,9 @@ def tile_scoremagnitudemetric_kernel(
         psum = ctx.enter_context(tc.psum_pool(name="psum", bufs=1))
         ctx.enter_context(tc.manual_schedule())
 
+        def f32(name, *shape):
+            return keep.tile([P] + list(shape), F32, name=name, align_bytes=64)
+
         w_codes = [keep.tile([P, PASSES, 2 * HALF], U8, name="w_codes%d" % h, align_bytes=64) for h in range(2)]
         w_plane = keep.tile([P, PASSES, N], U8, name="w_plane", align_bytes=64)
         pos_codes = [keep.tile([P, PASSES, POS], U8, name="pos_codes%d" % h, align_bytes=64) for h in range(2)]
@@ -69,27 +73,30 @@ def tile_scoremagnitudemetric_kernel(
         xdot_sb = [keep.tile([P, n, D], BF16, name="xdot%d" % c, align_bytes=64) for c, n in enumerate(XDOT_CHUNKS)]
         xdot_tile = [sb[:, j, :] for sb, n in zip(xdot_sb, XDOT_CHUNKS) for j in range(n)]
 
-        ident = keep.tile([P, P], F32, name="ident", align_bytes=64)
-        zeros = keep.tile([P, HALF // 2], F32, name="zeros", align_bytes=64)
-        result = keep.tile([P, P], F32, name="result", align_bytes=64)
-        warm = keep.tile([P, 1], F32, name="warm")
-        pos_ab = keep.tile([P, POS_TILES, 2], F32, name="pos_ab")
-        pos_st = keep.tile([P, POS_TILES, 6], F32, name="pos_st")
-        pos_q = keep.tile([P, POS_TILES, 2], F32, name="pos_q")
-        pos_pw = keep.tile([P, POS_TILES], F32, name="pos_pw")
-        ends = keep.tile([P, 2], F32, name="ends")
-        span = keep.tile([P, 4], F32, name="span")
-        ab = keep.tile([P, 2], F32, name="ab")
-        x_ab = keep.tile([P, X_TILES, 2], F32, name="x_ab")
-        x_st = keep.tile([P, len(V_TILES), 6], F32, name="x_st")
-        x_q = keep.tile([P, len(V_TILES), 2], F32, name="x_q")
-        x_end = keep.tile([P, 1], F32, name="x_end")
-        xd = keep.tile([P, X_TILES], F32, name="xd")
-        pw = keep.tile([P, X_TILES], F32, name="pw")
-        late_ax = keep.tile([P, N_LATE], F32, name="late_ax")
-        late_bx = keep.tile([P, N_LATE], F32, name="late_bx")
-        late_ss = keep.tile([P, N_LATE], F32, name="late_ss")
-        pw_last = keep.tile([P, 1], F32, name="pw_last")
+        ident = f32("ident", P)
+        zeros = f32("zeros", HALF // 2)
+        result = f32("result", P)
+        warm = f32("warm", 1)
+        pos_st = f32("pos_st", 2 * POS_TILES, 6)
+        pos_q = f32("pos_q", POS_TILES, 4)
+        pos_pw = f32("pos_pw", POS_TILES)
+        ends = f32("ends", 2)
+        span = f32("span", 2)
+        inv = f32("inv", 2)
+        drop = f32("drop", 1)
+        ab = f32("ab", 2)
+        x_end = f32("x_end", 2)
+        x_st = f32("x_st", 2 * LAST, 6)
+        x_q = f32("x_q", LATE, 4)
+        xd = f32("xd", X_TILES)
+        g_sq = [f32("g_sq%d" % k, D) for k in range(len(G_XDOT))]
+        g_sum = f32("g_sum", len(G_XDOT), FOLD)
+        pw = f32("pw", LATE)
+        late_ax = f32("late_ax", N_LATE)
+        late_bx = f32("late_bx", N_LATE)
+        late_q = f32("late_q", LAST - LATE, 4)
+        late_ss = f32("late_ss", LAST - LATE)
+        pw_last = f32("pw_last", 1)
         rows = keep.tile([X_TILES, P], F32, name="rows")
         alpha, beta = ab[:, 0:1], ab[:, 1:2]
 
@@ -98,7 +105,8 @@ def tile_scoremagnitudemetric_kernel(
         nc.vector.memset(pos_plane[:].rearrange("p g n -> p (g n)").bitcast(I32), 0)
         nc.vector.memset(warm[:], 1.0)
         nc.vector.memset(x_plane[:].rearrange("p g n -> p (g n)").bitcast(I32), 0)
-        nc.vector.memset(result[:], 0.0)
+        for part in (pos_st, x_st, result):
+            nc.vector.memset(part[:], 0.0)
         nc.scalar.activation(out=warm[:], in_=warm[:], func=ACT.Square)
 
         xdot_rows = x_dot.rearrange("(i p) d -> p i d", p=P)
@@ -123,17 +131,17 @@ def tile_scoremagnitudemetric_kernel(
             load_xdot(nc.gpsimd, c)
         make_identity(nc, ident[:])
 
-        def psum_s(n=HALF):
-            return psum.tile([P, n], F32, name="acc_s", bufs=5)
+        def bank_s():
+            return psum.tile([P, HALF], F32, name="acc_s", bufs=3)
 
-        def psum_v(shape):
-            return psum.tile(shape, F32, name="acc_v", bufs=3)
+        def bank_v(*shape):
+            return psum.tile([P] + list(shape), F32, name="acc_v", bufs=5)
 
-        idle = psum_v([P, HALF])
+        idle = bank_v(HALF)
         for k in range(WARM):
             nc.tensor.matmul(idle[:], zeros[:].bitcast(BF16)[:, 0:P], zeros[:].bitcast(BF16), start=True, stop=True)
 
-        def matmuls(step, h, acc, lo=0, n=HALF):
+        def matmuls(step, h, dst):
             if step < POS_TILES:
                 codes, plane, col, pcol = pos_codes[step // 4], pos_plane, step % 4, step
             else:
@@ -141,11 +149,11 @@ def tile_scoremagnitudemetric_kernel(
                 codes, plane, col, pcol = x_codes[t // 16], x_plane, t % 16, t
             for g in range(PASSES):
                 nc.tensor.matmul_mx(
-                    out=acc[:],
+                    out=dst[:],
                     lhsT=codes[:, g, 2 * P * col : 2 * P * (col + 1)].bitcast(FP4X4),
                     lhsT_scale=plane[:, g, P * pcol : P * (pcol + 1)],
-                    rhs=w_codes[h][:, g, 2 * lo : 2 * (lo + n)].bitcast(FP4X4),
-                    rhs_scale=w_plane[:, g, HALF * h + lo : HALF * h + lo + n],
+                    rhs=w_codes[h][:, g, :].bitcast(FP4X4),
+                    rhs_scale=w_plane[:, g, HALF * h : HALF * (h + 1)],
                     start=(g == 0),
                     stop=(g == PASSES - 1),
                 )
@@ -154,127 +162,129 @@ def tile_scoremagnitudemetric_kernel(
             junk = scrap.tile([P, D], BF16, name="junk_s")
             nc.scalar.activation(out=junk[:, 0 : src.shape[1]], in_=src, func=ACT.Square, accum_out=dst)
 
-        def vector_xdot(j):
-            junk = scrap.tile([P, D], F32, name="junk_v")
-            nc.vector.scalar_tensor_tensor(
-                out=junk[:], in0=xdot_tile[j], scalar=1.0, in1=xdot_tile[j], op0=ALU.mult, op1=ALU.mult,
-                accum_out=xd[:, j : j + 1],
-            )
+        def half(step, h):
+            t = step - POS_TILES
+            if t == LAST:
+                acc = bank_s()
+                matmuls(step, h, acc)
+                scalar_sumsq(acc[:], x_end[:, h : h + 1])
+                return
+            stats, row = (pos_st, 2 * step + h) if t < 0 else (x_st, 2 * t + h)
+            if h == 1 and (row // 2) % 3 == 1:
+                acc = bank_s()
+                matmuls(step, h, acc)
+                scalar_sumsq(acc[:], stats[:, row, 2:3])
+            else:
+                acc = bank_v(HALF)
+                matmuls(step, h, acc)
+                nc.vector.bn_stats(out=stats[:, row, :], in_=acc[:])
 
-        def scalar_half(step, h, dst, lo=0, n=HALF):
-            acc_s = psum_s(n)
-            matmuls(step, h, acc_s, lo, n)
-            scalar_sumsq(acc_s[:], dst)
+        gtt, gts = nc.gpsimd.tensor_tensor, nc.gpsimd.tensor_scalar
 
-        def vector_half(step, h, dst):
-            acc_v = psum_v([P, HALF])
-            matmuls(step, h, acc_v)
-            nc.vector.bn_stats(out=dst, in_=acc_v[:])
+        def gpsimd_xdot(k):
+            sq = g_sq[k]
+            gtt(out=sq[:], in0=xdot_tile[G_XDOT[k]], in1=xdot_tile[G_XDOT[k]], op=ALU.mult)
+            w = D // 2
+            while w >= FOLD:
+                dst = sq[:, 0:w] if w > FOLD else g_sum[:, k, :]
+                gtt(out=dst, in0=sq[:, 0:w], in1=sq[:, w : 2 * w], op=ALU.add)
+                w //= 2
 
-        tt = nc.vector.tensor_tensor
+        def gpsimd_fold():
+            w = FOLD // 2
+            while w >= 1:
+                dst = g_sum[:, :, 0:w] if w > 1 else xd[:, 0 : G_XDOT[-1] + 1 : 4].rearrange("p (k e) -> p k e", e=1)
+                gtt(out=dst, in0=g_sum[:, :, 0:w], in1=g_sum[:, :, w : 2 * w], op=ALU.add)
+                w //= 2
 
-        def sums_of_stats(stats, q, dst):
-            return [
-                lambda: tt(out=q, in0=stats[:, :, 1::3], in1=stats[:, :, 1::3], op=ALU.mult),
-                lambda: nc.vector.scalar_tensor_tensor(
-                    out=q, in0=q, scalar=float(HALF // 2), in1=stats[:, :, 2::3], op0=ALU.mult, op1=ALU.add
-                ),
-                lambda: tt(out=dst, in0=q[:, :, 0], in1=q[:, :, 1], op=ALU.add),
-            ]
-
-        def powers(sums, dst):
-            return [
-                lambda: tt(out=dst, in0=sums[:, :, 0], in1=sums[:, :, 1], op=ALU.add),
-                lambda: tt(out=dst, in0=dst, in1=dst, op=ALU.mult),
-            ]
-
-        chores = {}
-
-        def at(step, per_step, todo):
-            for k, chore in enumerate(todo):
-                chores.setdefault(step + k // per_step, []).append(chore)
+        def powers(stats, q, dst):
+            q2 = q[:].rearrange("p k (h e) -> p (k h) e", h=2)
+            gtt(out=q2, in0=stats[:, :, 1::3], in1=stats[:, :, 1::3], op=ALU.mult)
+            gts(out=q2, in0=q2, scalar1=float(HALF // 2), scalar2=0.0, op0=ALU.mult, op1=ALU.add)
+            gtt(out=q2, in0=q2, in1=stats[:, :, 2::3], op=ALU.add)
+            gtt(out=q[:, :, 0:2], in0=q[:, :, 0:2], in1=q[:, :, 2:4], op=ALU.add)
+            gtt(out=q[:, :, 0], in0=q[:, :, 0], in1=q[:, :, 1], op=ALU.add)
+            gtt(out=dst, in0=q[:, :, 0], in1=q[:, :, 0], op=ALU.mult)
 
         spread = {}
 
         def spread_ends():
-            spread[0] = psum_v([P, 2, P])
+            spread[0] = bank_v(2, P)
             for k in range(2):
                 nc.tensor.transpose(spread[0][:, k, :], ends[:, k : k + 1].to_broadcast([P, P]), ident[:])
 
-        at(8, 1, sums_of_stats(pos_st[:], pos_q[:], pos_ab[:, :, 1]) + powers(pos_ab[:], pos_pw[:]) + [
-            lambda: nc.vector.tensor_reduce(out=ends[:, 0:1], in_=pos_pw[:], axis=AX.X, op=ALU.max),
-            lambda: nc.vector.tensor_reduce(out=ends[:, 1:2], in_=pos_pw[:], axis=AX.X, op=ALU.min),
-        ])
-        at(CALIB_STEP, 1, [
-            lambda: nc.vector.tensor_reduce(out=span[:, 0:1], in_=spread[0][:, 0, :], axis=AX.X, op=ALU.max),
-            lambda: nc.vector.tensor_reduce(out=span[:, 1:2], in_=spread[0][:, 1, :], axis=AX.X, op=ALU.min),
-            lambda: tt(out=span[:, 2:3], in0=span[:, 0:1], in1=span[:, 1:2], op=ALU.subtract),
-            lambda: nc.vector.reciprocal(out=span[:, 3:4], in_=span[:, 2:3]),
-            lambda: nc.vector.tensor_scalar(out=alpha, in0=span[:, 3:4], scalar1=MAXI - MINI, scalar2=None, op0=ALU.mult),
-            lambda: tt(out=span[:, 2:3], in0=alpha, in1=span[:, 1:2], op=ALU.mult),
-            lambda: nc.vector.tensor_scalar(out=beta, in0=span[:, 2:3], scalar1=-1.0, scalar2=MINI, op0=ALU.mult, op1=ALU.add),
-        ])
-        at(35, 2, sums_of_stats(x_st[:], x_q[:], x_ab[:, 2:28:4, 1]) + [
-            lambda: nc.vector.tensor_scalar(out=late_ax[:], in0=xd[:, LATE:], scalar1=alpha, scalar2=None, op0=ALU.mult),
-            lambda: nc.vector.tensor_scalar(out=late_bx[:], in0=xd[:, LATE:], scalar1=beta, scalar2=None, op0=ALU.mult),
-        ])
-        at(37, 4, powers(x_ab[:, 0:LATE, :], pw[:, 0:LATE]) + [
-            lambda: nc.vector.tensor_scalar(
-                out=pw[:, 0:LATE], in0=pw[:, 0:LATE], scalar1=alpha, scalar2=beta, op0=ALU.mult, op1=ALU.add
-            ),
-            lambda: tt(out=result[:, 0:LATE], in0=pw[:, 0:LATE], in1=xd[:, 0:LATE], op=ALU.mult),
-        ])
+        def line():
+            gts(out=alpha, in0=inv[:, 1:2], scalar1=MAXI - MINI, scalar2=0.0, op0=ALU.mult, op1=ALU.add)
+            gtt(out=drop[:], in0=alpha, in1=span[:, 1:2], op=ALU.mult)
+            gts(out=beta, in0=drop[:], scalar1=-1.0, scalar2=MINI, op0=ALU.mult, op1=ALU.add)
 
-        def late_tile(t):
-            k = t - LATE
-            ss = late_ss[:, k : k + 1]
-            tt(out=ss, in0=x_ab[:, t, 0:1], in1=x_ab[:, t, 1:2], op=ALU.add)
-            if t < LAST:
-                nc.vector.scalar_tensor_tensor(out=ss, in0=ss, scalar=ss, in1=late_ax[:, k : k + 1], op0=ALU.mult, op1=ALU.mult)
-                tt(out=result[:, t : t + 1], in0=ss, in1=late_bx[:, k : k + 1], op=ALU.add)
+        def early_scores():
+            powers(x_st[:, 0 : 2 * LATE, :], x_q, pw[:])
+            gts(out=pw[:], in0=pw[:], scalar1=alpha, scalar2=beta, op0=ALU.mult, op1=ALU.add)
+            gtt(out=result[:, 0:LATE], in0=pw[:], in1=xd[:, 0:LATE], op=ALU.mult)
 
-        for j in S_XDOT:
-            scalar_sumsq(xdot_tile[j], xd[:, j : j + 1])
-        for j in V_XDOT[:2]:
-            vector_xdot(j)
+        def late_line():
+            gts(out=late_ax[:], in0=xd[:, LATE:], scalar1=alpha, scalar2=0.0, op0=ALU.mult, op1=ALU.add)
+            gts(out=late_bx[:], in0=xd[:, LATE:], scalar1=beta, scalar2=0.0, op0=ALU.mult, op1=ALU.add)
+
+        g_jobs = {
+            0: [lambda: gpsimd_xdot(0), lambda: gpsimd_xdot(1)],
+            7: [lambda: powers(pos_st[:], pos_q, pos_pw[:]), lambda: gpsimd_xdot(2), lambda: gpsimd_xdot(3)],
+            CALIB_STEP: [line, lambda: gpsimd_xdot(4), gpsimd_fold],
+            POS_TILES + LATE - 1: [early_scores],
+            36: [late_line],
+        }
+        v_jobs = {
+            20: [
+                lambda: nc.vector.tensor_reduce(out=ends[:, 0:1], in_=pos_pw[:], axis=AX.X, op=ALU.max),
+                lambda: nc.vector.tensor_reduce(out=ends[:, 1:2], in_=pos_pw[:], axis=AX.X, op=ALU.min),
+            ],
+            CALIB_STEP: [
+                lambda: nc.vector.tensor_reduce(out=span[:, 0:1], in_=spread[0][:, 0, :], axis=AX.X, op=ALU.max),
+                lambda: nc.vector.tensor_reduce(out=span[:, 1:2], in_=spread[0][:, 1, :], axis=AX.X, op=ALU.min),
+                lambda: nc.vector.tensor_scalar(out=inv[:, 0:1], in0=span[:, 0:1], scalar1=span[:, 1:2], scalar2=None, op0=ALU.subtract),
+                lambda: nc.vector.reciprocal(out=inv[:, 1:2], in_=inv[:, 0:1]),
+            ],
+        }
+
+        def late_scores():
+            stats = x_st[:, 2 * LATE :, :]
+            means, spreads = stats[:, :, 1::3], stats[:, :, 2::3]
+            q2 = late_q[:].rearrange("p k (h e) -> p (k h) e", h=2)
+            tt, stt = nc.vector.tensor_tensor, nc.vector.scalar_tensor_tensor
+            tt(out=q2, in0=means, in1=means, op=ALU.mult)
+            stt(out=q2, in0=q2, scalar=float(HALF // 2), in1=spreads, op0=ALU.mult, op1=ALU.add)
+            nc.vector.tensor_reduce(out=late_ss[:], in_=late_q[:], axis=AX.X, op=ALU.add)
+            tt(out=late_ss[:], in0=late_ss[:], in1=late_ss[:], op=ALU.mult)
+            tt(out=late_ss[:], in0=late_ss[:], in1=late_ax[:, 0 : LAST - LATE], op=ALU.mult)
+            tt(out=result[:, LATE:LAST], in0=late_ss[:], in1=late_bx[:, 0 : LAST - LATE], op=ALU.add)
+
         slots = {}
-        for k, j in enumerate(V_XDOT[2:6]):
-            slots.setdefault(1 + 2 * k, []).append(j)
-        for k, j in enumerate(V_XDOT[6:]):
-            slots.setdefault(8 + k * 27 // len(V_XDOT[6:]), []).append(j)
-
-        for step in range(4):
-            scalar_half(step, 0, pos_ab[:, step, 0:1])
+        for j in S_XDOT[:S_HEAD]:
+            scalar_sumsq(xdot_tile[j], xd[:, j : j + 1])
+        for k, j in enumerate(S_XDOT[S_HEAD:]):
+            slots.setdefault(1 + k * 3 // 2, []).append(j)
+        for step in range(3):
+            half(step, 0)
         for step in range(STEPS):
-            t = step - POS_TILES
             if step == CALIB_STEP:
                 spread_ends()
-            if t < 0:
-                if step >= 4:
-                    scalar_half(step, 0, pos_ab[:, step, 0:1])
-                vector_half(step, 1, pos_st[:, step, :])
-            else:
-                scalar_half(step, 0, x_ab[:, t, 0:1])
-                if t in V_TILES:
-                    vector_half(step, 1, x_st[:, V_TILES.index(t), :])
-                elif t < LAST:
-                    scalar_half(step, 1, x_ab[:, t, 1:2])
-                else:
-                    scalar_half(step, 1, x_ab[:, t, 1:2], 0, HALF // 2)
-                    scalar_half(step, 1, x_end[:], HALF // 2, HALF // 2)
+            if step >= 3:
+                half(step, 0)
+            half(step, 1)
             for j in slots.get(step, []):
-                vector_xdot(j)
-            for chore in chores.get(step, []):
-                chore()
-            if t >= LATE:
-                late_tile(t)
+                scalar_sumsq(xdot_tile[j], xd[:, j : j + 1])
+            for jobs in (v_jobs, g_jobs):
+                for job in jobs.get(step, []):
+                    job()
+        late_scores()
         k = N_LATE - 1
-        nc.scalar.activation(out=pw_last[:], in_=x_end[:], func=ACT.Square, bias=late_ss[:, k : k + 1])
+        nc.scalar.activation(out=pw_last[:], in_=x_end[:, 1:2], func=ACT.Square, bias=x_end[:, 0:1])
         nc.scalar.activation(
             out=result[:, LAST : LAST + 1], in_=pw_last[:], func=ACT.Identity,
             scale=late_ax[:, k : k + 1], bias=late_bx[:, k : k + 1],
         )
-        turned = psum_v([P, P])
+        turned = bank_v(P)
         nc.tensor.transpose(turned[:], result[:], ident[:])
         nc.scalar.copy(out=rows[:], in_=turned[0:X_TILES, :])
         nc.scalar.dma_start(out=out.rearrange("(i p) -> i p", p=P), in_=rows[:])

from contextlib import ExitStack

import concourse.mybir as mybir
from concourse.masks import make_identity

F32 = mybir.dt.float32
BF16 = mybir.dt.bfloat16
I32 = mybir.dt.int32
U8 = mybir.dt.uint8
FP4X4 = mybir.dt.float4_e2m1fn_x4
ALU = mybir.AluOpType
ACT = mybir.ActivationFunctionType
AX = mybir.AxisListType

P = 128
D = 1024
N = 1024
B = 4096
POS = 1024
PASSES = 2
HALF = 512
MINI, MAXI = 0.001, 1.0
FLOPS = 2 * (B + POS) * D * N + 2 * (B + POS) * N + 2 * B * D

POS_TILES = POS // P
X_TILES = B // P
STEPS = POS_TILES + X_TILES
LAST = X_TILES - 1
LATE = 24
N_LATE = X_TILES - LATE
X_CHUNK = 2048
XDOT_CHUNKS = [2, 2, 4, 4, 4, 4, 4, 4, 4]
GPSIMD_CHUNKS = 3
CALIB_STEP = 24
WARM = 9
FOLD = 32
G_XDOT = [0, 4, 8, 12, 16]
S_XDOT = [j for j in range(X_TILES) if j not in G_XDOT]
S_HEAD = 3


def load_scales(nc, plane, scales):
    for q in range(4):
        nc.sync.dma_start(
            out=plane[32 * q : 32 * q + 4, :, :].bitcast(I32),
            in_=scales[:, 4 * q : 4 * q + 4, :].rearrange("g r n -> r g n").bitcast(I32),
        )


def load_codes(nc, codes, words):
    nc.sync.dma_start(out=codes[:].bitcast(I32), in_=words.rearrange("g p n -> p g n").bitcast(I32))


def tile_scoremagnitudemetric_kernel(
    tc, x_words, x_scales, x_dot, pos_words, pos_scales, w_words, w_scales, out
):
    nc = tc.nc
    with ExitStack() as ctx:
        keep = ctx.enter_context(tc.tile_pool(name="keep", bufs=1))
        scrap = ctx.enter_context(tc.tile_pool(name="scrap", bufs=3))
        psum = ctx.enter_context(tc.psum_pool(name="psum", bufs=1))
        ctx.enter_context(tc.manual_schedule())

        def f32(name, *shape):
            return keep.tile([P] + list(shape), F32, name=name, align_bytes=64)

        w_codes = [keep.tile([P, PASSES, 2 * HALF], U8, name="w_codes%d" % h, align_bytes=64) for h in range(2)]
        w_plane = keep.tile([P, PASSES, N], U8, name="w_plane", align_bytes=64)
        pos_codes = [keep.tile([P, PASSES, POS], U8, name="pos_codes%d" % h, align_bytes=64) for h in range(2)]
        pos_plane = keep.tile([P, PASSES, POS], U8, name="pos_plane", align_bytes=64)
        x_codes = [keep.tile([P, PASSES, 2 * X_CHUNK], U8, name="x_codes%d" % c, align_bytes=64) for c in range(2)]
        x_plane = keep.tile([P, PASSES, B], U8, name="x_plane", align_bytes=64)
        xdot_sb = [keep.tile([P, n, D], BF16, name="xdot%d" % c, align_bytes=64) for c, n in enumerate(XDOT_CHUNKS)]
        xdot_tile = [sb[:, j, :] for sb, n in zip(xdot_sb, XDOT_CHUNKS) for j in range(n)]

        ident = f32("ident", P)
        zeros = f32("zeros", HALF // 2)
        result = f32("result", P)
        warm = f32("warm", 1)
        pos_st = f32("pos_st", 2 * POS_TILES, 6)
        pos_q = f32("pos_q", POS_TILES, 4)
        pos_pw = f32("pos_pw", POS_TILES)
        ends = f32("ends", 2)
        span = f32("span", 2)
        inv = f32("inv", 2)
        drop = f32("drop", 1)
        ab = f32("ab", 2)
        x_end = f32("x_end", 2)
        x_st = f32("x_st", 2 * LAST, 6)
        x_q = f32("x_q", LATE, 4)
        xd = f32("xd", X_TILES)
        g_sq = [f32("g_sq%d" % k, D) for k in range(len(G_XDOT))]
        g_sum = f32("g_sum", len(G_XDOT), FOLD)
        pw = f32("pw", LATE)
        late_ax = f32("late_ax", N_LATE)
        late_bx = f32("late_bx", N_LATE)
        late_q = f32("late_q", LAST - LATE, 4)
        late_ss = f32("late_ss", LAST - LATE)
        pw_last = f32("pw_last", 1)
        rows = keep.tile([X_TILES, P], F32, name="rows")
        alpha, beta = ab[:, 0:1], ab[:, 1:2]

        nc.gpsimd.memset(zeros[:], 0.0)
        nc.vector.memset(w_plane[:].rearrange("p g n -> p (g n)").bitcast(I32), 0)
        nc.vector.memset(pos_plane[:].rearrange("p g n -> p (g n)").bitcast(I32), 0)
        nc.vector.memset(warm[:], 1.0)
        nc.vector.memset(x_plane[:].rearrange("p g n -> p (g n)").bitcast(I32), 0)
        for part in (pos_st, x_st, result):
            nc.vector.memset(part[:], 0.0)
        nc.scalar.activation(out=warm[:], in_=warm[:], func=ACT.Square)

        xdot_rows = x_dot.rearrange("(i p) d -> p i d", p=P)
        first = [sum(XDOT_CHUNKS[:c]) for c in range(len(XDOT_CHUNKS))]

        def load_xdot(eng, c):
            eng.dma_start(out=xdot_sb[c][:], in_=xdot_rows[:, first[c] : first[c] + XDOT_CHUNKS[c], :])

        load_codes(nc, w_codes[0], w_words[:, :, 0 : 2 * HALF])
        load_codes(nc, pos_codes[0], pos_words[:, :, 0:POS])
        load_scales(nc, w_plane, w_scales)
        load_scales(nc, pos_plane, pos_scales)
        load_codes(nc, w_codes[1], w_words[:, :, 2 * HALF :])
        load_codes(nc, pos_codes[1], pos_words[:, :, POS:])
        load_scales(nc, x_plane, x_scales)
        load_codes(nc, x_codes[0], x_words[:, :, 0 : 2 * X_CHUNK])
        load_xdot(nc.sync, GPSIMD_CHUNKS)
        load_codes(nc, x_codes[1], x_words[:, :, 2 * X_CHUNK :])
        for c in range(GPSIMD_CHUNKS + 1, len(XDOT_CHUNKS)):
            load_xdot(nc.sync, c)
        for c in range(GPSIMD_CHUNKS):
            load_xdot(nc.gpsimd, c)
        make_identity(nc, ident[:])

        def bank_s():
            return psum.tile([P, HALF], F32, name="acc_s", bufs=3)

        def bank_v(*shape):
            return psum.tile([P] + list(shape), F32, name="acc_v", bufs=5)

        idle = bank_v(HALF)
        for k in range(WARM):
            nc.tensor.matmul(idle[:], zeros[:].bitcast(BF16)[:, 0:P], zeros[:].bitcast(BF16), start=True, stop=True)

        def matmuls(step, h, dst):
            if step < POS_TILES:
                codes, plane, col, pcol = pos_codes[step // 4], pos_plane, step % 4, step
            else:
                t = step - POS_TILES
                codes, plane, col, pcol = x_codes[t // 16], x_plane, t % 16, t
            for g in range(PASSES):
                nc.tensor.matmul_mx(
                    out=dst[:],
                    lhsT=codes[:, g, 2 * P * col : 2 * P * (col + 1)].bitcast(FP4X4),
                    lhsT_scale=plane[:, g, P * pcol : P * (pcol + 1)],
                    rhs=w_codes[h][:, g, :].bitcast(FP4X4),
                    rhs_scale=w_plane[:, g, HALF * h : HALF * (h + 1)],
                    start=(g == 0),
                    stop=(g == PASSES - 1),
                )

        def scalar_sumsq(src, dst):
            junk = scrap.tile([P, D], BF16, name="junk_s")
            nc.scalar.activation(out=junk[:, 0 : src.shape[1]], in_=src, func=ACT.Square, accum_out=dst)

        def half(step, h):
            t = step - POS_TILES
            if t == LAST:
                acc = bank_s()
                matmuls(step, h, acc)
                scalar_sumsq(acc[:], x_end[:, h : h + 1])
                return
            stats, row = (pos_st, 2 * step + h) if t < 0 else (x_st, 2 * t + h)
            if h == 1 and (row // 2) % 3 == 1:
                acc = bank_s()
                matmuls(step, h, acc)
                scalar_sumsq(acc[:], stats[:, row, 2:3])
            else:
                acc = bank_v(HALF)
                matmuls(step, h, acc)
                nc.vector.bn_stats(out=stats[:, row, :], in_=acc[:])

        gtt, gts = nc.gpsimd.tensor_tensor, nc.gpsimd.tensor_scalar

        def gpsimd_xdot(k):
            sq = g_sq[k]
            gtt(out=sq[:], in0=xdot_tile[G_XDOT[k]], in1=xdot_tile[G_XDOT[k]], op=ALU.mult)
            w = D // 2
            while w >= FOLD:
                dst = sq[:, 0:w] if w > FOLD else g_sum[:, k, :]
                gtt(out=dst, in0=sq[:, 0:w], in1=sq[:, w : 2 * w], op=ALU.add)
                w //= 2

        def gpsimd_fold():
            w = FOLD // 2
            while w >= 1:
                dst = g_sum[:, :, 0:w] if w > 1 else xd[:, 0 : G_XDOT[-1] + 1 : 4].rearrange("p (k e) -> p k e", e=1)
                gtt(out=dst, in0=g_sum[:, :, 0:w], in1=g_sum[:, :, w : 2 * w], op=ALU.add)
                w //= 2

        def powers(stats, q, dst):
            q2 = q[:].rearrange("p k (h e) -> p (k h) e", h=2)
            gtt(out=q2, in0=stats[:, :, 1::3], in1=stats[:, :, 1::3], op=ALU.mult)
            gts(out=q2, in0=q2, scalar1=float(HALF // 2), scalar2=0.0, op0=ALU.mult, op1=ALU.add)
            gtt(out=q2, in0=q2, in1=stats[:, :, 2::3], op=ALU.add)
            gtt(out=q[:, :, 0:2], in0=q[:, :, 0:2], in1=q[:, :, 2:4], op=ALU.add)
            gtt(out=q[:, :, 0], in0=q[:, :, 0], in1=q[:, :, 1], op=ALU.add)
            gtt(out=dst, in0=q[:, :, 0], in1=q[:, :, 0], op=ALU.mult)

        spread = {}

        def spread_ends():
            spread[0] = bank_v(2, P)
            for k in range(2):
                nc.tensor.transpose(spread[0][:, k, :], ends[:, k : k + 1].to_broadcast([P, P]), ident[:])

        def line():
            gts(out=alpha, in0=inv[:, 1:2], scalar1=MAXI - MINI, scalar2=0.0, op0=ALU.mult, op1=ALU.add)
            gtt(out=drop[:], in0=alpha, in1=span[:, 1:2], op=ALU.mult)
            gts(out=beta, in0=drop[:], scalar1=-1.0, scalar2=MINI, op0=ALU.mult, op1=ALU.add)

        def early_scores():
            powers(x_st[:, 0 : 2 * LATE, :], x_q, pw[:])
            gts(out=pw[:], in0=pw[:], scalar1=alpha, scalar2=beta, op0=ALU.mult, op1=ALU.add)
            gtt(out=result[:, 0:LATE], in0=pw[:], in1=xd[:, 0:LATE], op=ALU.mult)

        def late_line():
            gts(out=late_ax[:], in0=xd[:, LATE:], scalar1=alpha, scalar2=0.0, op0=ALU.mult, op1=ALU.add)
            gts(out=late_bx[:], in0=xd[:, LATE:], scalar1=beta, scalar2=0.0, op0=ALU.mult, op1=ALU.add)

        g_jobs = {
            0: [lambda: gpsimd_xdot(0), lambda: gpsimd_xdot(1)],
            7: [lambda: powers(pos_st[:], pos_q, pos_pw[:]), lambda: gpsimd_xdot(2), lambda: gpsimd_xdot(3)],
            CALIB_STEP: [line, lambda: gpsimd_xdot(4), gpsimd_fold],
            POS_TILES + LATE - 1: [early_scores],
            36: [late_line],
        }
        v_jobs = {
            20: [
                lambda: nc.vector.tensor_reduce(out=ends[:, 0:1], in_=pos_pw[:], axis=AX.X, op=ALU.max),
                lambda: nc.vector.tensor_reduce(out=ends[:, 1:2], in_=pos_pw[:], axis=AX.X, op=ALU.min),
            ],
            CALIB_STEP: [
                lambda: nc.vector.tensor_reduce(out=span[:, 0:1], in_=spread[0][:, 0, :], axis=AX.X, op=ALU.max),
                lambda: nc.vector.tensor_reduce(out=span[:, 1:2], in_=spread[0][:, 1, :], axis=AX.X, op=ALU.min),
                lambda: nc.vector.tensor_scalar(out=inv[:, 0:1], in0=span[:, 0:1], scalar1=span[:, 1:2], scalar2=None, op0=ALU.subtract),
                lambda: nc.vector.reciprocal(out=inv[:, 1:2], in_=inv[:, 0:1]),
            ],
        }

        def late_scores():
            stats = x_st[:, 2 * LATE :, :]
            means, spreads = stats[:, :, 1::3], stats[:, :, 2::3]
            q2 = late_q[:].rearrange("p k (h e) -> p (k h) e", h=2)
            tt, stt = nc.vector.tensor_tensor, nc.vector.scalar_tensor_tensor
            tt(out=q2, in0=means, in1=means, op=ALU.mult)
            stt(out=q2, in0=q2, scalar=float(HALF // 2), in1=spreads, op0=ALU.mult, op1=ALU.add)
            nc.vector.tensor_reduce(out=late_ss[:], in_=late_q[:], axis=AX.X, op=ALU.add)
            tt(out=late_ss[:], in0=late_ss[:], in1=late_ss[:], op=ALU.mult)
            tt(out=late_ss[:], in0=late_ss[:], in1=late_ax[:, 0 : LAST - LATE], op=ALU.mult)
            tt(out=result[:, LATE:LAST], in0=late_ss[:], in1=late_bx[:, 0 : LAST - LATE], op=ALU.add)

        slots = {}
        for j in S_XDOT[:S_HEAD]:
            scalar_sumsq(xdot_tile[j], xd[:, j : j + 1])
        for k, j in enumerate(S_XDOT[S_HEAD:]):
            slots.setdefault(1 + k * 3 // 2, []).append(j)
        for step in range(3):
            half(step, 0)
        for step in range(STEPS):
            if step == CALIB_STEP:
                spread_ends()
            if step >= 3:
                half(step, 0)
            half(step, 1)
            for j in slots.get(step, []):
                scalar_sumsq(xdot_tile[j], xd[:, j : j + 1])
            for jobs in (v_jobs, g_jobs):
                for job in jobs.get(step, []):
                    job()
        late_scores()
        k = N_LATE - 1
        nc.scalar.activation(out=pw_last[:], in_=x_end[:, 1:2], func=ACT.Square, bias=x_end[:, 0:1])
        nc.scalar.activation(
            out=result[:, LAST : LAST + 1], in_=pw_last[:], func=ACT.Identity,
            scale=late_ax[:, k : k + 1], bias=late_bx[:, k : k + 1],
        )
        turned = bank_v(P)
        nc.tensor.transpose(turned[:], result[:], ident[:])
        nc.scalar.copy(out=rows[:], in_=turned[0:X_TILES, :])
        nc.scalar.dma_start(out=out.rearrange("(i p) -> i p", p=P), in_=rows[:])
